import numpy as np
import ml_dtypes


def mxq(x, axis, fmt="e4m3"):
    dtype, down = {"e4m3": (ml_dtypes.float8_e4m3fn, 7), "e5m2": (ml_dtypes.float8_e5m2, 14)}[fmt]
    v = np.moveaxis(np.asarray(x, np.float32).astype(ml_dtypes.bfloat16).astype(np.float64), axis, -1)
    blocks = v.reshape(v.shape[:-1] + (-1, 32))
    amax = np.abs(blocks).max(-1, keepdims=True)
    byte = np.maximum(np.where(amax > 0, np.frexp(amax)[1] - 1 + 127, 0) - down, 1)
    scale = np.exp2(byte - 127.0)
    codes = (blocks / scale).astype(np.float32).astype(dtype).astype(np.float64)
    return np.moveaxis((codes * scale).reshape(v.shape), -1, axis)


WIDE = False


def mx_kscale(k):
    if not WIDE:
        return np.ones(k)
    levels = np.array([10, -10, 5, -5, 0])
    if k % 512:
        return np.exp2(np.random.permutation(np.resize(levels, k // 32))).repeat(32)
    a = np.empty((k // 512, 16))
    for p in range(k // 512):
        a[p, :8] = np.random.permutation(np.resize(levels, 8))
        for g in range(8):
            far = levels[np.abs(levels - a[p, g]) >= 10]
            a[p, g + 8] = far[np.random.randint(len(far))]
    return np.exp2(a.ravel()).repeat(32)


BF16 = ml_dtypes.bfloat16


def bf(x):
    return np.asarray(x, np.float32).astype(BF16)


def f64(x):
    return np.asarray(x).astype(np.float64)


N, M0, D0, M1, D1, M2, D2 = 1536, 512, 1, 512, 3, 256, 5
IRREPS = [(M0, D0), (M1, D1), (M2, D2)]
IN_DIM = sum(m * d for m, d in IRREPS)


def setup_inputs():
    s0, s1 = mx_kscale(M0), mx_kscale(M1)
    sx = np.concatenate([np.repeat(s0, D0), np.repeat(s1, D1), np.ones(M2 * D2)])
    return {"x": bf(np.random.standard_normal((N, IN_DIM)) * sx),
            "w0": bf(np.random.standard_normal((M0, M0)) * 0.4 / s0[:, None]),
            "w1": bf(np.random.standard_normal((M1, M1)) * 0.4 / s1[:, None]),
            "w2": bf(np.random.standard_normal((M2, M2)) * 0.4)}


def reference(x, w0, w1, w2):
    x = f64(x)
    outs = []
    off = 0
    for (mul, d), w, quantised in zip(IRREPS, [f64(w0), f64(w1), f64(w2)], [True, True, False]):
        blk = x[:, off:off + mul * d].reshape(N, mul, d)
        if quantised:
            y = mxq(blk, 1, "e4m3").transpose(0, 2, 1) @ mxq(w, 0, "e4m3")
        else:
            y = blk.transpose(0, 2, 1) @ w
        y = (1.0 / np.sqrt(mul)) * y.transpose(0, 2, 1)
        outs.append(y.reshape(N, mul * d))
        off += mul * d
    return np.concatenate(outs, axis=-1)

@@ -1,0 +1,224 @@
+from contextlib import ExitStack
+import math
+
+import concourse.mybir as mybir
+from concourse.masks import make_identity
+
+FP8X4 = mybir.dt.float8_e4m3fn_x4
+BF16 = mybir.dt.bfloat16
+F32 = mybir.dt.float32
+U32 = mybir.dt.uint32
+U8 = mybir.dt.uint8
+MULT = mybir.AluOpType.mult
+ADD = mybir.AluOpType.add
+
+P = 128
+ROWS = 1536
+TILES = ROWS // P
+COLS = 3328
+MUL01 = 512
+D1 = 3
+OFF1 = 512
+MUL2 = 256
+D2 = 5
+OFF2 = 2048
+PAIRS = COLS // 2
+BANK = 512
+OPERANDS = 1 + D1
+SCALE01 = 1.0 / math.sqrt(MUL01)
+SCALE2 = 1.0 / math.sqrt(MUL2)
+LOAD_GROUPS = [1, 1, 2, 4, 4]
+CHUNKS2 = [(0, 88), (88, 88), (176, 80)]
+CHUNK1 = 128
+
+FLOPS = 2 * ROWS * (MUL01 * MUL01 * (1 + D1) + MUL2 * MUL2 * D2)
+
+
+def tile_linear_kernel(tc, x, w0, w1, w2, out):
+    nc = tc.nc
+    x_rows = x.rearrange("(p t) c -> p (t c)", t=TILES)
+    out_rows = out.rearrange("(p t) c -> p (t c)", t=TILES)
+
+    def vector_scaled(dst, src, factor):
+        nc.vector.tensor_scalar(out=dst, in0=src, scalar1=factor, scalar2=None, op0=MULT)
+
+    def scalar_scaled(dst, src, factor):
+        nc.scalar.mul(dst, src, factor)
+
+    drain1 = [scalar_scaled, vector_scaled, scalar_scaled, scalar_scaled]
+    drain2 = [scalar_scaled, vector_scaled, scalar_scaled]
+
+    with ExitStack() as ctx:
+        keep = ctx.enter_context(tc.tile_pool(name="keep", bufs=1))
+        stage = ctx.enter_context(tc.tile_pool(name="stage", bufs=3))
+        outs = ctx.enter_context(tc.tile_pool(name="outs", bufs=5))
+        psum = ctx.enter_context(tc.psum_pool(name="psum", bufs=8))
+        ctx.enter_context(tc.manual_schedule())
+
+        ident = keep.tile([P, P], F32, name="ident")
+        make_identity(nc, ident[:])
+
+        x_tiles = []
+        x_loads = []
+        first = 0
+        for g, count in enumerate(LOAD_GROUPS):
+            x_sb = keep.tile([P, count * COLS], BF16, name="x%d" % g)
+            x_loads.append((x_sb, first, count))
+            for k in range(count):
+                x_tiles.append((x_sb, k))
+            first += count
+
+        def load_x(g):
+            x_sb, start, count = x_loads[g]
+            nc.sync.dma_start(out=x_sb[:], in_=x_rows[:, start * COLS:(start + count) * COLS])
+
+        def load_mx_weight(name, w):
+            raw = keep.tile([P, 4, MUL01], BF16, name="raw_" + name)
+            nc.sync.dma_start(out=raw[:], in_=w.rearrange("(p j) c -> p j c", j=4))
+            return raw
+
+        load_x(0)
+        raw1 = load_mx_weight("w1", w1)
+        raw0 = load_mx_weight("w0", w0)
+        w2_sb = keep.tile([P, 2, MUL2], BF16, name="w2_sb")
+        nc.sync.dma_start(out=w2_sb[:], in_=w2.rearrange("(m e) c -> m e c", e=2))
+        for g in range(1, len(LOAD_GROUPS)):
+            load_x(g)
+
+        def mx_weight_tiles(name):
+            grouped = keep.tile([P, MUL01, 4], BF16, name="grp_" + name, align_bytes=64)
+            codes = keep.tile([P, MUL01], U32, name="codes_" + name, align_bytes=64)
+            scales = keep.tile([P, MUL01], U8, name="scales_" + name, align_bytes=64)
+            return grouped, codes, scales
+
+        grouped1, codes1, scales1 = mx_weight_tiles("w1")
+        grouped0, codes0, scales0 = mx_weight_tiles("w0")
+
+        def quantise(grouped_flat, codes, scales):
+            nc.vector.quantize_mx(out=codes[:].bitcast(FP8X4), scales=scales[:], in_=grouped_flat)
+
+        sorted1 = {}
+        mx_operands = {}
+        plain_operands = {}
+
+        def sort_block1(t):
+            x_sb, k = x_tiles[t]
+            by_component = stage.tile([P, D1 * MUL01], BF16, name="xs1")
+            sorted1[t] = by_component
+            nc.gpsimd.tensor_scalar(
+                out=by_component[:].rearrange("p (i u) -> p i u", i=D1),
+                in0=x_sb[:, k * COLS + OFF1:k * COLS + OFF2].rearrange("p (u i) -> p i u", i=D1),
+                scalar1=1.0,
+                scalar2=0.0,
+                op0=MULT,
+                op1=ADD,
+            )
+
+        def transposes(t):
+            x_sb, k = x_tiles[t]
+            pairs = x_sb[:].bitcast(F32)[:, k * PAIRS:(k + 1) * PAIRS]
+            pairs1 = sorted1[t][:].bitcast(F32)
+
+            x2T = stage.tile([P, 2 * D2 * P], BF16, name="xT2")
+            plain_operands[t] = x2T
+            bank_a = psum.tile([P, BANK], F32, name="tb2", tag="bank")
+            for r in range(4):
+                nc.tensor.transpose(bank_a[:, r * P:(r + 1) * P], pairs[:, OFF2 // 2 + r:PAIRS:D2], ident[:])
+            bank_b = psum.tile([P, BANK], F32, name="tb3", tag="bank")
+            nc.tensor.transpose(bank_b[:, 0:P], pairs[:, OFF2 // 2 + 4:PAIRS:D2], ident[:])
+            nc.scalar.copy(
+                x2T[:, 0:8 * P].rearrange("p (r e n) -> p r e n", r=4, e=2),
+                bank_a[:].bitcast(BF16).rearrange("p (r n e) -> p r e n", r=4, e=2),
+            )
+            nc.vector.tensor_copy(
+                out=x2T[:, 8 * P:10 * P].rearrange("p (e n) -> p e n", e=2),
+                in_=bank_b[:].bitcast(BF16)[:, 0:2 * P].rearrange("p (n e) -> p e n", e=2),
+            )
+
+            grouped = stage.tile([P, OPERANDS * P * 4], BF16, name="grouped", align_bytes=64)
+            grouped_pairs = grouped[:].bitcast(F32)
+            for b in range(OPERANDS // 2):
+                bank = psum.tile([P, BANK], F32, name="tb01", tag="bank")
+                for s in (2 * b, 2 * b + 1):
+                    for h in range(2):
+                        if s == 0:
+                            src = pairs[:, h:2 * P:2]
+                        else:
+                            src = pairs1[:, 2 * (s - 1) * P + h:2 * s * P:2]
+                        q = 2 * (s - 2 * b) + h
+                        nc.tensor.transpose(bank[:, q * P:(q + 1) * P], src, ident[:])
+                nc.vector.tensor_copy(
+                    out=grouped_pairs[:, b * BANK:(b + 1) * BANK].rearrange("p (s n h) -> p s n h", s=2, h=2),
+                    in_=bank[:].rearrange("p (s h n) -> p s n h", s=2, h=2),
+                )
+            codes = stage.tile([P, OPERANDS * P], U32, name="codes", align_bytes=64)
+            scales = stage.tile([P, OPERANDS * P], U8, name="scales", align_bytes=64)
+            mx_operands[t] = (grouped, codes, scales)
+
+        def quantise_x(t):
+            grouped, codes, scales = mx_operands[t]
+            quantise(grouped[:], codes, scales)
+
+        def products(t):
+            grouped, codes, scales = mx_operands[t]
+            x2T = plain_operands[t]
+            o = outs.tile([P, COLS], F32, name="o")
+
+            def mx_pass(acc, s, w_codes, w_scales):
+                nc.tensor.matmul_mx(
+                    out=acc,
+                    lhsT=codes[:, s * P:(s + 1) * P].bitcast(FP8X4),
+                    lhsT_scale=scales[:, s * P:(s + 1) * P],
+                    rhs=w_codes.bitcast(FP8X4),
+                    rhs_scale=w_scales,
+                    start=True,
+                    stop=True,
+                )
+
+            for c in range(MUL01 // CHUNK1):
+                cols = slice(c * CHUNK1, (c + 1) * CHUNK1)
+                acc1 = psum.tile([P, BANK], F32, name="acc1", tag="bank")
+                for i in range(D1):
+                    mx_pass(acc1[:, i * CHUNK1:(i + 1) * CHUNK1], 1 + i, codes1[:, cols], scales1[:, cols])
+                lo = OFF1 + c * D1 * CHUNK1
+                drain1[c](
+                    o[:, lo:lo + D1 * CHUNK1].rearrange("p (w i) -> p w i", i=D1),
+                    acc1[:, 0:D1 * CHUNK1].rearrange("p (i w) -> p w i", i=D1),
+                    SCALE01,
+                )
+                if c == 1 and t + 1 < TILES:
+                    quantise_x(t + 1)
+            acc0 = psum.tile([P, BANK], F32, name="acc0", tag="bank")
+            mx_pass(acc0[:], 0, codes0[:], scales0[:])
+            vector_scaled(o[:, 0:OFF1], acc0[:], SCALE01)
+            for c, (w_lo, w_n) in enumerate(CHUNKS2):
+                acc2 = psum.tile([P, BANK], F32, name="acc2", tag="bank")
+                for i in range(D2):
+                    for e2 in range(2):
+                        f = D2 * e2 + i
+                        nc.tensor.matmul(
+                            out=acc2[:, i * w_n:(i + 1) * w_n],
+                            lhsT=x2T[:, f * P:(f + 1) * P],
+                            rhs=w2_sb[:, e2, w_lo:w_lo + w_n],
+                            start=(e2 == 0),
+                            stop=(e2 == 1),
+                        )
+                drain2[c](
+                    o[:, OFF2 + D2 * w_lo:OFF2 + D2 * (w_lo + w_n)].rearrange("p (w i) -> p w i", i=D2),
+                    acc2[:, 0:D2 * w_n].rearrange("p (i w) -> p w i", i=D2),
+                    SCALE2,
+                )
+            nc.sync.dma_start(out=out_rows[:, t * COLS:(t + 1) * COLS], in_=o[:])
+
+        sort_block1(0)
+        nc.vector.tensor_copy(out=grouped1[:], in_=raw1[:].rearrange("p t c -> p c t"))
+        transposes(0)
+        nc.scalar.copy(grouped0[:], raw0[:].rearrange("p t c -> p c t"))
+        quantise(grouped1[:].rearrange("p c t -> p (c t)"), codes1, scales1)
+        quantise_x(0)
+        quantise(grouped0[:].rearrange("p c t -> p (c t)"), codes0, scales0)
+        for t in range(TILES):
+            if t + 1 < TILES:
+                sort_block1(t + 1)
+                transposes(t + 1)
+            products(t)

@@ -27,6 +27,7 @@ BANK = 512
 OPERANDS = 1 + D1
 SCALE01 = 1.0 / math.sqrt(MUL01)
 SCALE2 = 1.0 / math.sqrt(MUL2)
+DMA_ALIGN = 256
 LOAD_GROUPS = [1, 1, 2, 4, 4]
 CHUNKS2 = [(0, 88), (88, 88), (176, 80)]
 CHUNK1 = 128
@@ -62,7 +63,7 @@ def tile_linear_kernel(tc, x, w0, w1, w2, out):
         x_loads = []
         first = 0
         for g, count in enumerate(LOAD_GROUPS):
-            x_sb = keep.tile([P, count * COLS], BF16, name="x%d" % g)
+            x_sb = keep.tile([P, count * COLS], BF16, name="x%d" % g, align_bytes=DMA_ALIGN)
             x_loads.append((x_sb, first, count))
             for k in range(count):
                 x_tiles.append((x_sb, k))
@@ -73,14 +74,14 @@ def tile_linear_kernel(tc, x, w0, w1, w2, out):
             nc.sync.dma_start(out=x_sb[:], in_=x_rows[:, start * COLS:(start + count) * COLS])
 
         def load_mx_weight(name, w):
-            raw = keep.tile([P, 4, MUL01], BF16, name="raw_" + name)
+            raw = keep.tile([P, 4, MUL01], BF16, name="raw_" + name, align_bytes=DMA_ALIGN)
             nc.sync.dma_start(out=raw[:], in_=w.rearrange("(p j) c -> p j c", j=4))
             return raw
 
         load_x(0)
         raw1 = load_mx_weight("w1", w1)
         raw0 = load_mx_weight("w0", w0)
-        w2_sb = keep.tile([P, 2, MUL2], BF16, name="w2_sb")
+        w2_sb = keep.tile([P, 2, MUL2], BF16, name="w2_sb", align_bytes=DMA_ALIGN)
         nc.sync.dma_start(out=w2_sb[:], in_=w2.rearrange("(m e) c -> m e c", e=2))
         for g in range(1, len(LOAD_GROUPS)):
             load_x(g)
@@ -162,7 +163,7 @@ def tile_linear_kernel(tc, x, w0, w1, w2, out):
         def products(t):
             grouped, codes, scales = mx_operands[t]
             x2T = plain_operands[t]
-            o = outs.tile([P, COLS], F32, name="o")
+            o = outs.tile([P, COLS], F32, name="o", align_bytes=DMA_ALIGN)
 
             def mx_pass(acc, s, w_codes, w_scales):
                 nc.tensor.matmul_mx(

@@ -106,14 +106,12 @@ def tile_linear_kernel(tc, x, w0, w1, w2, out):
             x_sb, k = x_tiles[t]
             by_component = stage.tile([P, D1 * MUL01], BF16, name="xs1")
             sorted1[t] = by_component
-            nc.gpsimd.tensor_scalar(
-                out=by_component[:].rearrange("p (i u) -> p i u", i=D1),
-                in0=x_sb[:, k * COLS + OFF1:k * COLS + OFF2].rearrange("p (u i) -> p i u", i=D1),
-                scalar1=1.0,
-                scalar2=0.0,
-                op0=MULT,
-                op1=ADD,
-            )
+            placed = by_component[:].rearrange("p (i h m e) -> p h i m e", i=D1, h=2, e=2)
+            as_loaded = x_sb[:, k * COLS + OFF1:k * COLS + OFF2].rearrange("p (m h e i) -> p h i m e", i=D1, h=2, e=2)
+            for h in range(2):
+                nc.gpsimd.tensor_scalar(
+                    out=placed[:, h], in0=as_loaded[:, h], scalar1=1.0, scalar2=0.0, op0=MULT, op1=ADD
+                )
 
         def transposes(t):
             x_sb, k = x_tiles[t]
@@ -145,7 +143,7 @@ def tile_linear_kernel(tc, x, w0, w1, w2, out):
                         if s == 0:
                             src = pairs[:, h:2 * P:2]
                         else:
-                            src = pairs1[:, 2 * (s - 1) * P + h:2 * s * P:2]
+                            src = pairs1[:, (2 * (s - 1) + h) * P:(2 * (s - 1) + h + 1) * P]
                         q = 2 * (s - 2 * b) + h
                         nc.tensor.transpose(bank[:, q * P:(q + 1) * P], src, ident[:])
                 nc.vector.tensor_copy(

@@ -29,6 +29,7 @@ SCALE01 = 1.0 / math.sqrt(MUL01)
 SCALE2 = 1.0 / math.sqrt(MUL2)
 DMA_ALIGN = 256
 LOAD_GROUPS = [1, 1, 2, 4, 4]
+STORE_GROUPS = [2, 2, 2, 2, 2, 1, 1]
 CHUNKS2 = [(0, 88), (88, 88), (176, 80)]
 CHUNK1 = 128
 
@@ -52,7 +53,7 @@ def tile_linear_kernel(tc, x, w0, w1, w2, out):
     with ExitStack() as ctx:
         keep = ctx.enter_context(tc.tile_pool(name="keep", bufs=1))
         stage = ctx.enter_context(tc.tile_pool(name="stage", bufs=3))
-        outs = ctx.enter_context(tc.tile_pool(name="outs", bufs=5))
+        outs = ctx.enter_context(tc.tile_pool(name="outs", bufs=3))
         psum = ctx.enter_context(tc.psum_pool(name="psum", bufs=8))
         ctx.enter_context(tc.manual_schedule())
 
@@ -158,10 +159,9 @@ def tile_linear_kernel(tc, x, w0, w1, w2, out):
             grouped, codes, scales = mx_operands[t]
             quantise(grouped[:], codes, scales)
 
-        def products(t):
+        def products(t, o):
             grouped, codes, scales = mx_operands[t]
             x2T = plain_operands[t]
-            o = outs.tile([P, COLS], F32, name="o", align_bytes=DMA_ALIGN)
 
             def mx_pass(acc, s, w_codes, w_scales):
                 nc.tensor.matmul_mx(
@@ -207,7 +207,6 @@ def tile_linear_kernel(tc, x, w0, w1, w2, out):
                     acc2[:, 0:D2 * w_n].rearrange("p (i w) -> p w i", i=D2),
                     SCALE2,
                 )
-            nc.sync.dma_start(out=out_rows[:, t * COLS:(t + 1) * COLS], in_=o[:])
 
         sort_block1(0)
         nc.vector.tensor_copy(out=grouped1[:], in_=raw1[:].rearrange("p t c -> p c t"))
@@ -216,8 +215,14 @@ def tile_linear_kernel(tc, x, w0, w1, w2, out):
         quantise(grouped1[:].rearrange("p c t -> p (c t)"), codes1, scales1)
         quantise_x(0)
         quantise(grouped0[:].rearrange("p c t -> p (c t)"), codes0, scales0)
-        for t in range(TILES):
-            if t + 1 < TILES:
-                sort_block1(t + 1)
-                transposes(t + 1)
-            products(t)
+        t = 0
+        for count in STORE_GROUPS:
+            o_sb = outs.tile([P, count * COLS], F32, name="o", align_bytes=DMA_ALIGN)
+            start = t
+            for k in range(count):
+                if t + 1 < TILES:
+                    sort_block1(t + 1)
+                    transposes(t + 1)
+                products(t, o_sb[:, k * COLS:(k + 1) * COLS])
+                t += 1
+            nc.sync.dma_start(out=out_rows[:, start * COLS:t * COLS], in_=o_sb[:])

from contextlib import ExitStack
import math

import concourse.mybir as mybir
from concourse.masks import make_identity

FP8X4 = mybir.dt.float8_e4m3fn_x4
BF16 = mybir.dt.bfloat16
F32 = mybir.dt.float32
U32 = mybir.dt.uint32
U8 = mybir.dt.uint8
MULT = mybir.AluOpType.mult
ADD = mybir.AluOpType.add

P = 128
ROWS = 1536
TILES = ROWS // P
COLS = 3328
MUL01 = 512
D1 = 3
OFF1 = 512
MUL2 = 256
D2 = 5
OFF2 = 2048
PAIRS = COLS // 2
BANK = 512
OPERANDS = 1 + D1
SCALE01 = 1.0 / math.sqrt(MUL01)
SCALE2 = 1.0 / math.sqrt(MUL2)
DMA_ALIGN = 256
LOAD_GROUPS = [1, 1, 2, 4, 4]
STORE_GROUPS = [2, 2, 2, 2, 2, 1, 1]
CHUNKS2 = [(0, 88), (88, 88), (176, 80)]
CHUNK1 = 128

FLOPS = 2 * ROWS * (MUL01 * MUL01 * (1 + D1) + MUL2 * MUL2 * D2)


def tile_linear_kernel(tc, x, w0, w1, w2, out):
    nc = tc.nc
    x_rows = x.rearrange("(p t) c -> p (t c)", t=TILES)
    out_rows = out.rearrange("(p t) c -> p (t c)", t=TILES)

    def vector_scaled(dst, src, factor):
        nc.vector.tensor_scalar(out=dst, in0=src, scalar1=factor, scalar2=None, op0=MULT)

    def scalar_scaled(dst, src, factor):
        nc.scalar.mul(dst, src, factor)

    drain1 = [scalar_scaled, vector_scaled, scalar_scaled, scalar_scaled]
    drain2 = [scalar_scaled, vector_scaled, scalar_scaled]

    with ExitStack() as ctx:
        keep = ctx.enter_context(tc.tile_pool(name="keep", bufs=1))
        stage = ctx.enter_context(tc.tile_pool(name="stage", bufs=3))
        outs = ctx.enter_context(tc.tile_pool(name="outs", bufs=3))
        psum = ctx.enter_context(tc.psum_pool(name="psum", bufs=8))
        ctx.enter_context(tc.manual_schedule())

        ident = keep.tile([P, P], F32, name="ident")
        make_identity(nc, ident[:])

        x_tiles = []
        x_loads = []
        first = 0
        for g, count in enumerate(LOAD_GROUPS):
            x_sb = keep.tile([P, count * COLS], BF16, name="x%d" % g, align_bytes=DMA_ALIGN)
            x_loads.append((x_sb, first, count))
            for k in range(count):
                x_tiles.append((x_sb, k))
            first += count

        def load_x(g):
            x_sb, start, count = x_loads[g]
            nc.sync.dma_start(out=x_sb[:], in_=x_rows[:, start * COLS:(start + count) * COLS])

        def load_mx_weight(name, w):
            raw = keep.tile([P, 4, MUL01], BF16, name="raw_" + name, align_bytes=DMA_ALIGN)
            nc.sync.dma_start(out=raw[:], in_=w.rearrange("(p j) c -> p j c", j=4))
            return raw

        load_x(0)
        raw1 = load_mx_weight("w1", w1)
        raw0 = load_mx_weight("w0", w0)
        w2_sb = keep.tile([P, 2, MUL2], BF16, name="w2_sb", align_bytes=DMA_ALIGN)
        nc.sync.dma_start(out=w2_sb[:], in_=w2.rearrange("(m e) c -> m e c", e=2))
        for g in range(1, len(LOAD_GROUPS)):
            load_x(g)

        def mx_weight_tiles(name):
            grouped = keep.tile([P, MUL01, 4], BF16, name="grp_" + name, align_bytes=64)
            codes = keep.tile([P, MUL01], U32, name="codes_" + name, align_bytes=64)
            scales = keep.tile([P, MUL01], U8, name="scales_" + name, align_bytes=64)
            return grouped, codes, scales

        grouped1, codes1, scales1 = mx_weight_tiles("w1")
        grouped0, codes0, scales0 = mx_weight_tiles("w0")

        def quantise(grouped_flat, codes, scales):
            nc.vector.quantize_mx(out=codes[:].bitcast(FP8X4), scales=scales[:], in_=grouped_flat)

        sorted1 = {}
        mx_operands = {}
        plain_operands = {}

        def sort_block1(t):
            x_sb, k = x_tiles[t]
            by_component = stage.tile([P, D1 * MUL01], BF16, name="xs1")
            sorted1[t] = by_component
            placed = by_component[:].rearrange("p (i h m e) -> p h i m e", i=D1, h=2, e=2)
            as_loaded = x_sb[:, k * COLS + OFF1:k * COLS + OFF2].rearrange("p (m h e i) -> p h i m e", i=D1, h=2, e=2)
            for h in range(2):
                nc.gpsimd.tensor_scalar(
                    out=placed[:, h], in0=as_loaded[:, h], scalar1=1.0, scalar2=0.0, op0=MULT, op1=ADD
                )

        def transposes(t):
            x_sb, k = x_tiles[t]
            pairs = x_sb[:].bitcast(F32)[:, k * PAIRS:(k + 1) * PAIRS]
            pairs1 = sorted1[t][:].bitcast(F32)

            x2T = stage.tile([P, 2 * D2 * P], BF16, name="xT2")
            plain_operands[t] = x2T
            bank_a = psum.tile([P, BANK], F32, name="tb2", tag="bank")
            for r in range(4):
                nc.tensor.transpose(bank_a[:, r * P:(r + 1) * P], pairs[:, OFF2 // 2 + r:PAIRS:D2], ident[:])
            bank_b = psum.tile([P, BANK], F32, name="tb3", tag="bank")
            nc.tensor.transpose(bank_b[:, 0:P], pairs[:, OFF2 // 2 + 4:PAIRS:D2], ident[:])
            nc.scalar.copy(
                x2T[:, 0:8 * P].rearrange("p (r e n) -> p r e n", r=4, e=2),
                bank_a[:].bitcast(BF16).rearrange("p (r n e) -> p r e n", r=4, e=2),
            )
            nc.vector.tensor_copy(
                out=x2T[:, 8 * P:10 * P].rearrange("p (e n) -> p e n", e=2),
                in_=bank_b[:].bitcast(BF16)[:, 0:2 * P].rearrange("p (n e) -> p e n", e=2),
            )

            grouped = stage.tile([P, OPERANDS * P * 4], BF16, name="grouped", align_bytes=64)
            grouped_pairs = grouped[:].bitcast(F32)
            for b in range(OPERANDS // 2):
                bank = psum.tile([P, BANK], F32, name="tb01", tag="bank")
                for s in (2 * b, 2 * b + 1):
                    for h in range(2):
                        if s == 0:
                            src = pairs[:, h:2 * P:2]
                        else:
                            src = pairs1[:, (2 * (s - 1) + h) * P:(2 * (s - 1) + h + 1) * P]
                        q = 2 * (s - 2 * b) + h
                        nc.tensor.transpose(bank[:, q * P:(q + 1) * P], src, ident[:])
                nc.vector.tensor_copy(
                    out=grouped_pairs[:, b * BANK:(b + 1) * BANK].rearrange("p (s n h) -> p s n h", s=2, h=2),
                    in_=bank[:].rearrange("p (s h n) -> p s n h", s=2, h=2),
                )
            codes = stage.tile([P, OPERANDS * P], U32, name="codes", align_bytes=64)
            scales = stage.tile([P, OPERANDS * P], U8, name="scales", align_bytes=64)
            mx_operands[t] = (grouped, codes, scales)

        def quantise_x(t):
            grouped, codes, scales = mx_operands[t]
            quantise(grouped[:], codes, scales)

        def products(t, o):
            grouped, codes, scales = mx_operands[t]
            x2T = plain_operands[t]

            def mx_pass(acc, s, w_codes, w_scales):
                nc.tensor.matmul_mx(
                    out=acc,
                    lhsT=codes[:, s * P:(s + 1) * P].bitcast(FP8X4),
                    lhsT_scale=scales[:, s * P:(s + 1) * P],
                    rhs=w_codes.bitcast(FP8X4),
                    rhs_scale=w_scales,
                    start=True,
                    stop=True,
                )

            for c in range(MUL01 // CHUNK1):
                cols = slice(c * CHUNK1, (c + 1) * CHUNK1)
                acc1 = psum.tile([P, BANK], F32, name="acc1", tag="bank")
                for i in range(D1):
                    mx_pass(acc1[:, i * CHUNK1:(i + 1) * CHUNK1], 1 + i, codes1[:, cols], scales1[:, cols])
                lo = OFF1 + c * D1 * CHUNK1
                drain1[c](
                    o[:, lo:lo + D1 * CHUNK1].rearrange("p (w i) -> p w i", i=D1),
                    acc1[:, 0:D1 * CHUNK1].rearrange("p (i w) -> p w i", i=D1),
                    SCALE01,
                )
                if c == 1 and t + 1 < TILES:
                    quantise_x(t + 1)
            acc0 = psum.tile([P, BANK], F32, name="acc0", tag="bank")
            mx_pass(acc0[:], 0, codes0[:], scales0[:])
            vector_scaled(o[:, 0:OFF1], acc0[:], SCALE01)
            for c, (w_lo, w_n) in enumerate(CHUNKS2):
                acc2 = psum.tile([P, BANK], F32, name="acc2", tag="bank")
                for i in range(D2):
                    for e2 in range(2):
                        f = D2 * e2 + i
                        nc.tensor.matmul(
                            out=acc2[:, i * w_n:(i + 1) * w_n],
                            lhsT=x2T[:, f * P:(f + 1) * P],
                            rhs=w2_sb[:, e2, w_lo:w_lo + w_n],
                            start=(e2 == 0),
                            stop=(e2 == 1),
                        )
                drain2[c](
                    o[:, OFF2 + D2 * w_lo:OFF2 + D2 * (w_lo + w_n)].rearrange("p (w i) -> p w i", i=D2),
                    acc2[:, 0:D2 * w_n].rearrange("p (i w) -> p w i", i=D2),
                    SCALE2,
                )

        sort_block1(0)
        nc.vector.tensor_copy(out=grouped1[:], in_=raw1[:].rearrange("p t c -> p c t"))
        transposes(0)
        nc.scalar.copy(grouped0[:], raw0[:].rearrange("p t c -> p c t"))
        quantise(grouped1[:].rearrange("p c t -> p (c t)"), codes1, scales1)
        quantise_x(0)
        quantise(grouped0[:].rearrange("p c t -> p (c t)"), codes0, scales0)
        t = 0
        for count in STORE_GROUPS:
            o_sb = outs.tile([P, count * COLS], F32, name="o", align_bytes=DMA_ALIGN)
            start = t
            for k in range(count):
                if t + 1 < TILES:
                    sort_block1(t + 1)
                    transposes(t + 1)
                products(t, o_sb[:, k * COLS:(k + 1) * COLS])
                t += 1
            nc.sync.dma_start(out=out_rows[:, start * COLS:t * COLS], in_=o_sb[:])
